import numpy as np
import ml_dtypes


def mxq(x, axis, fmt="e4m3"):
    dtype, down = {"e4m3": (ml_dtypes.float8_e4m3fn, 7), "e5m2": (ml_dtypes.float8_e5m2, 14)}[fmt]
    v = np.moveaxis(np.asarray(x, np.float32).astype(ml_dtypes.bfloat16).astype(np.float64), axis, -1)
    blocks = v.reshape(v.shape[:-1] + (-1, 32))
    amax = np.abs(blocks).max(-1, keepdims=True)
    byte = np.maximum(np.where(amax > 0, np.frexp(amax)[1] - 1 + 127, 0) - down, 1)
    scale = np.exp2(byte - 127.0)
    codes = (blocks / scale).astype(np.float32).astype(dtype).astype(np.float64)
    return np.moveaxis((codes * scale).reshape(v.shape), -1, axis)


WIDE = False


def mx_kscale(k):
    if not WIDE:
        return np.ones(k)
    levels = np.array([10, -10, 5, -5, 0])
    if k % 512:
        return np.exp2(np.random.permutation(np.resize(levels, k // 32))).repeat(32)
    a = np.empty((k // 512, 16))
    for p in range(k // 512):
        a[p, :8] = np.random.permutation(np.resize(levels, 8))
        for g in range(8):
            far = levels[np.abs(levels - a[p, g]) >= 10]
            a[p, g + 8] = far[np.random.randint(len(far))]
    return np.exp2(a.ravel()).repeat(32)


BF16 = ml_dtypes.bfloat16


def bf(x):
    return np.asarray(x, np.float32).astype(BF16)


def f64(x):
    return np.asarray(x).astype(np.float64)


B, G, DB, DR = 512, 16, 512, 1024


def mish(v):
    return v * np.tanh(np.log(1.0 + np.exp(v)))


def setup_inputs():
    s, t = mx_kscale(DR), mx_kscale(DB)
    return {"BB_feature": bf(np.random.standard_normal((B, G, DB)) * t),
            "RF_feature": bf(np.random.standard_normal((B, DR)) * s),
            "W_bbbb": bf(np.random.standard_normal((DB, DB)) / np.sqrt(DB) / t),
            "b_bbbb": bf(np.random.standard_normal(DB) * 0.5),
            "W_rfbb": bf(np.random.standard_normal((DB, DR)) / np.sqrt(DR) / s),
            "b_rfbb": bf(np.random.standard_normal(DB) * 0.5)}


def reference(BB_feature, RF_feature, W_bbbb, b_bbbb, W_rfbb, b_rfbb):
    RF_to_BB = mish((mxq(f64(RF_feature), 1, "e4m3") @ mxq(f64(W_rfbb), 1, "e4m3").T) + f64(b_rfbb))
    BB_to_BB = mish((mxq(f64(BB_feature), 2, "e4m3") @ mxq(f64(W_bbbb), 1, "e4m3").T) + f64(b_bbbb))
    return BB_to_BB + RF_to_BB[:, None, :]

@@ -1,0 +1,279 @@
+from contextlib import ExitStack
+
+import concourse.mybir as mybir
+from concourse.masks import make_identity
+
+F32 = mybir.dt.float32
+BF16 = mybir.dt.bfloat16
+U32 = mybir.dt.uint32
+U8 = mybir.dt.uint8
+FP8X4 = mybir.dt.float8_e4m3fn_x4
+ACT = mybir.ActivationFunctionType
+ALU = mybir.AluOpType
+
+B, G, DB, DR = 512, 16, 512, 1024
+FLOPS = 2 * B * G * DB * DB + 2 * B * DR * DB
+
+P = 128
+PACK = 4
+K_PASS = P * PACK
+BLOCKS = 4
+CHUNK = BLOCKS * P
+HALF = BLOCKS // 2
+
+GROUP_SIZES = (10, 5, 2)
+
+LEAD = 4
+
+GUARD = 2.0 ** -60
+
+
+def tile_gnn_layer_pb_t_kernel(
+    tc, BB_feature, RF_feature, W_bbbb, b_bbbb, W_rfbb, b_rfbb, out
+):
+    nc = tc.nc
+    with ExitStack() as ctx:
+        consts = ctx.enter_context(tc.tile_pool(name="consts", bufs=1))
+        keep = ctx.enter_context(tc.tile_pool(name="keep", bufs=1))
+        raws = ctx.enter_context(tc.tile_pool(name="raws", bufs=4))
+        groupeds = ctx.enter_context(tc.tile_pool(name="groupeds", bufs=4))
+        acts = ctx.enter_context(tc.tile_pool(name="acts", bufs=13))
+        stages = ctx.enter_context(tc.tile_pool(name="stages", bufs=8))
+        front = ctx.enter_context(tc.psum_pool(name="front", bufs=4))
+        rest = ctx.enter_context(tc.psum_pool(name="rest", bufs=4))
+        ctx.enter_context(tc.manual_schedule())
+
+        ident = consts.tile([P, P], F32, name="ident")
+        make_identity(nc, ident[:])
+        guard = consts.tile([P, 1], F32, name="guard")
+        nc.vector.memset(guard[:], GUARD)
+        scratch = consts.tile([P, 1], F32, name="scratch")
+
+        def call_in_sigmoid_table():
+            nc.scalar.activation(out=scratch[:], in_=guard[:], func=ACT.Sigmoid)
+
+        call_in_sigmoid_table()
+
+        bias_rows = consts.tile([P, P], BF16, name="bias_rows")
+        nc.vector.memset(bias_rows[:], 0.0)
+        nc.sync.dma_start(
+            out=bias_rows[0:BLOCKS, :], in_=b_bbbb.rearrange("(o p) -> o p", p=P)
+        )
+        nc.sync.dma_start(
+            out=bias_rows[BLOCKS : 2 * BLOCKS, :], in_=b_rfbb.rearrange("(o p) -> o p", p=P)
+        )
+        bias_rows_f32 = consts.tile([P, P], F32, name="bias_rows_f32")
+        nc.vector.tensor_copy(out=bias_rows_f32[:], in_=bias_rows[:])
+        bias_bank = rest.tile([P, CHUNK], F32, name="bank")
+        nc.tensor.transpose(bias_bank[:, 0:P], bias_rows_f32[:], ident[:])
+        bias = consts.tile([P, 2 * BLOCKS], F32, name="bias")
+        nc.vector.tensor_copy(out=bias[:], in_=bias_bank[:, 0 : 2 * BLOCKS])
+        neg_bias = consts.tile([P, 2 * BLOCKS], F32, name="neg_bias")
+        nc.vector.tensor_scalar_mul(out=neg_bias[:], in0=bias[:], scalar1=-1.0)
+
+        rf_to_bb = consts.tile([P, BLOCKS, DB], F32, name="rf_to_bb")
+
+        def new_operand(label, passes):
+            codes = keep.tile([P, passes, CHUNK], U32, name="codes_" + label, align_bytes=64)
+            scales = keep.tile([P, passes, CHUNK], U8, name="scales_" + label, align_bytes=64)
+            return {"codes": codes, "scales": scales, "passes": passes}
+
+        def regroup(rows, scalar_helps):
+            raw = raws.tile([P, BLOCKS, K_PASS], BF16, name="raw")
+            nc.sync.dma_start(out=raw[:], in_=rows)
+            words = raw[:].bitcast(F32)
+            grouped = groupeds.tile([P, CHUNK * PACK], BF16, name="grouped", align_bytes=64)
+            grouped_words = grouped[:].bitcast(F32).rearrange(
+                "p (j r u) -> p j r u", j=BLOCKS, u=2
+            )
+            for h in range(HALF):
+                bank = rest.tile([P, CHUNK], F32, name="bank")
+                flipped = bank[:].rearrange("p (j u r) -> p j u r", j=2, u=2)
+                for j in range(2):
+                    for u in range(2):
+                        nc.tensor.transpose(
+                            flipped[:, j, u, :],
+                            words[:, 2 * h + j, u : 2 * P : 2],
+                            ident[:],
+                        )
+                copy = nc.scalar.copy if scalar_helps and h == 1 else nc.vector.tensor_copy
+                copy(
+                    out=grouped_words[:, 2 * h : 2 * h + 2, :, :],
+                    in_=flipped.rearrange("p j u r -> p j r u"),
+                )
+            return grouped
+
+        def quantise(operand, c, grouped):
+            nc.vector.quantize_mx(
+                out=operand["codes"][:, c, :].bitcast(FP8X4),
+                scales=operand["scales"][:, c, :],
+                in_=grouped[:],
+            )
+
+        def product(bank, chunk, o):
+            w, x = chunk["w"], chunk["x"]
+            cols = slice(o * P, (o + 1) * P)
+            for c in range(x["passes"]):
+                nc.tensor.matmul_mx(
+                    out=bank[:],
+                    lhsT=w["codes"][:, c, cols].bitcast(FP8X4),
+                    lhsT_scale=w["scales"][:, c, cols],
+                    rhs=x["codes"][:, c, :].bitcast(FP8X4),
+                    rhs_scale=x["scales"][:, c, :],
+                    start=(c == 0),
+                    stop=(c == x["passes"] - 1),
+                )
+
+        def sigmoid(chunk):
+            act = acts.tile([P, BLOCKS, CHUNK], F32, name="act")
+            chunk["act"] = act
+            for o in range(BLOCKS):
+                bank = front.tile([P, CHUNK], F32, name="first")
+                product(bank, chunk, o)
+                col = chunk["bias"] + o
+                nc.scalar.activation(
+                    out=act[:, o, :],
+                    in_=bank[:],
+                    func=ACT.Sigmoid,
+                    bias=neg_bias[:, col : col + 1],
+                    scale=-1.0,
+                )
+
+        def log(chunk):
+            act = chunk["act"]
+            nc.scalar.activation(
+                out=act[:], in_=act[:], func=ACT.Ln, bias=guard[:, 0:1], scale=1.0
+            )
+
+        def tanh(chunk):
+            act = chunk["act"]
+            for h in range(HALF):
+                half = act[:, 2 * h : 2 * h + 2, :]
+                nc.scalar.activation(out=half, in_=half, func=ACT.Tanh, scale=-1.0)
+
+        def times_z(chunk, h):
+            act = chunk["act"]
+            for o in range(2 * h, 2 * h + 2):
+                bank = rest.tile([P, CHUNK], F32, name="bank")
+                product(bank, chunk, o)
+                col = chunk["bias"] + o
+                nc.vector.scalar_tensor_tensor(
+                    out=act[:, o, :],
+                    in0=bank[:],
+                    scalar=bias[:, col : col + 1],
+                    in1=act[:, o, :],
+                    op0=ALU.add,
+                    op1=ALU.mult,
+                )
+
+        def turn_back(chunk, h):
+            act = chunk["act"]
+            for j in range(2 * h, 2 * h + 2):
+                bank = rest.tile([P, CHUNK], F32, name="bank")
+                for o in range(BLOCKS):
+                    nc.tensor.transpose(
+                        bank[:, o * P : (o + 1) * P], act[:, o, j * P : (j + 1) * P], ident[:]
+                    )
+                if chunk["sample_block"] is None:
+                    nc.vector.tensor_copy(out=rf_to_bb[:, j, :], in_=bank[:])
+                else:
+                    s = chunk["sample_block"]
+                    stage = stages.tile([P, DB], F32, name="stage")
+                    nc.vector.tensor_tensor(
+                        out=stage[:], in0=bank[:], in1=rf_to_bb[:, s, :], op=ALU.add
+                    )
+                    nc.sync.dma_start(
+                        out=out[s * P : (s + 1) * P, chunk["first_group"] + j, :], in_=stage[:]
+                    )
+
+        w_bb = new_operand("w_bb", 1)
+        w_rf = new_operand("w_rf", DR // K_PASS)
+        x_rf = new_operand("x_rf", DR // K_PASS)
+        w_bb_rows = W_bbbb.rearrange("(j p) k -> p j k", p=P)
+        w_rf_rows = W_rfbb.rearrange("(j p) k -> p j k", p=P)
+        x_rf_rows = RF_feature.rearrange("(j p) k -> p j k", p=P)
+
+        rf_chunk = {"x": x_rf, "w": w_rf, "bias": BLOCKS, "sample_block": None}
+        rf_passes = []
+        for c in range(DR // K_PASS):
+            k_cols = slice(c * K_PASS, (c + 1) * K_PASS)
+            rf_passes.append((w_rf, c, w_rf_rows[:, :, k_cols]))
+            rf_passes.append((x_rf, c, x_rf_rows[:, :, k_cols]))
+
+        bb_chunks = []
+        for n in range(B * G // CHUNK):
+            s, g0 = n // (G // BLOCKS), BLOCKS * (n % (G // BLOCKS))
+            bb_chunks.append(
+                {
+                    "x": new_operand("x_bb%d" % n, 1),
+                    "w": w_bb,
+                    "bias": 0,
+                    "sample_block": s,
+                    "first_group": g0,
+                }
+            )
+
+        def bb_pass(chunk):
+            s, g0 = chunk["sample_block"], chunk["first_group"]
+            return (chunk["x"], 0, BB_feature[s * P : (s + 1) * P, g0 : g0 + BLOCKS, :])
+
+        n_first = GROUP_SIZES[0] - 1
+        groups = [[rf_chunk] + bb_chunks[:n_first]]
+        start = n_first
+        for size in GROUP_SIZES[1:]:
+            groups.append(bb_chunks[start : start + size])
+            start += size
+        assert start == len(bb_chunks)
+
+        passes = [(w_bb, 0, w_bb_rows)]
+        passes.extend([bb_pass(chunk) for chunk in bb_chunks[:n_first]])
+        passes.extend(rf_passes)
+        passes.extend([bb_pass(chunk) for chunk in bb_chunks[n_first:]])
+
+        def written_before(i):
+            return min(len(passes), LEAD + i + i // 3)
+
+        state = {"pending": None}
+
+        def quantise_pending():
+            if state["pending"] is not None:
+                quantise(*state["pending"])
+                state["pending"] = None
+
+        def prepare(k, scalar_helps=False):
+            operand, c, rows = passes[k]
+            grouped = regroup(rows, scalar_helps)
+            quantise_pending()
+            state["pending"] = (operand, c, grouped)
+
+        prepare(0, scalar_helps=True)
+        prepare(1, scalar_helps=True)
+        quantise_pending()
+        done = 2
+        for i, chunk in enumerate(bb_chunks[:n_first] + [rf_chunk]):
+            for k in range(done, written_before(i)):
+                prepare(k)
+            done = written_before(i)
+            sigmoid(chunk)
+        assert done > 1 + n_first + len(rf_passes)
+        for k in range(done, len(passes)):
+            prepare(k)
+        quantise_pending()
+
+        for g, group in enumerate(groups):
+            following = groups[g + 1] if g + 1 < len(groups) else []
+            for chunk in group:
+                log(chunk)
+            call_in_sigmoid_table()
+            previous = None
+            for i, chunk in enumerate(group):
+                tanh(chunk)
+                if i < len(following):
+                    sigmoid(following[i])
+                for h in range(HALF):
+                    times_z(chunk, h)
+                    if previous is not None:
+                        turn_back(previous, h)
+                previous = chunk
+            for h in range(HALF):
+                turn_back(previous, h)

@@ -1,3 +1,4 @@
+import math
 from contextlib import ExitStack
 
 import concourse.mybir as mybir
@@ -21,7 +22,10 @@ BLOCKS = 4
 CHUNK = BLOCKS * P
 HALF = BLOCKS // 2
 
-GROUP_SIZES = (10, 5, 2)
+GROUP_SIZES = (12, 4)
+
+KEPT = ((0, 3, 6, 9), (1,))
+KEPT_DELAY = 3
 
 LEAD = 4
 
@@ -35,8 +39,6 @@ def tile_gnn_layer_pb_t_kernel(
     with ExitStack() as ctx:
         consts = ctx.enter_context(tc.tile_pool(name="consts", bufs=1))
         keep = ctx.enter_context(tc.tile_pool(name="keep", bufs=1))
-        raws = ctx.enter_context(tc.tile_pool(name="raws", bufs=4))
-        groupeds = ctx.enter_context(tc.tile_pool(name="groupeds", bufs=4))
         acts = ctx.enter_context(tc.tile_pool(name="acts", bufs=13))
         stages = ctx.enter_context(tc.tile_pool(name="stages", bufs=8))
         front = ctx.enter_context(tc.psum_pool(name="front", bufs=4))
@@ -47,6 +49,14 @@ def tile_gnn_layer_pb_t_kernel(
         make_identity(nc, ident[:])
         guard = consts.tile([P, 1], F32, name="guard")
         nc.vector.memset(guard[:], GUARD)
+        bias_rows = consts.tile([P, P], BF16, name="bias_rows")
+        nc.vector.memset(bias_rows[:], 0.0)
+        bias_rows_f32 = consts.tile([P, P], F32, name="bias_rows_f32")
+        bias = consts.tile([P, 2 * BLOCKS], F32, name="bias")
+        neg_bias = consts.tile([P, 2 * BLOCKS], F32, name="neg_bias")
+        steep_bias = consts.tile([P, 2 * BLOCKS], F32, name="steep_bias")
+        rf_to_bb = consts.tile([P, BLOCKS, DB], F32, name="rf_to_bb")
+        steep = consts.tile([P, BLOCKS, CHUNK], F32, name="steep")
         scratch = consts.tile([P, 1], F32, name="scratch")
 
         def call_in_sigmoid_table():
@@ -54,61 +64,59 @@ def tile_gnn_layer_pb_t_kernel(
 
         call_in_sigmoid_table()
 
-        bias_rows = consts.tile([P, P], BF16, name="bias_rows")
-        nc.vector.memset(bias_rows[:], 0.0)
-        nc.sync.dma_start(
-            out=bias_rows[0:BLOCKS, :], in_=b_bbbb.rearrange("(o p) -> o p", p=P)
-        )
-        nc.sync.dma_start(
-            out=bias_rows[BLOCKS : 2 * BLOCKS, :], in_=b_rfbb.rearrange("(o p) -> o p", p=P)
-        )
-        bias_rows_f32 = consts.tile([P, P], F32, name="bias_rows_f32")
-        nc.vector.tensor_copy(out=bias_rows_f32[:], in_=bias_rows[:])
-        bias_bank = rest.tile([P, CHUNK], F32, name="bank")
-        nc.tensor.transpose(bias_bank[:, 0:P], bias_rows_f32[:], ident[:])
-        bias = consts.tile([P, 2 * BLOCKS], F32, name="bias")
-        nc.vector.tensor_copy(out=bias[:], in_=bias_bank[:, 0 : 2 * BLOCKS])
-        neg_bias = consts.tile([P, 2 * BLOCKS], F32, name="neg_bias")
-        nc.vector.tensor_scalar_mul(out=neg_bias[:], in0=bias[:], scalar1=-1.0)
+        def load_biases():
+            nc.sync.dma_start(
+                out=bias_rows[0:BLOCKS, :], in_=b_bbbb.rearrange("(o p) -> o p", p=P)
+            )
+            nc.sync.dma_start(
+                out=bias_rows[BLOCKS : 2 * BLOCKS, :], in_=b_rfbb.rearrange("(o p) -> o p", p=P)
+            )
 
-        rf_to_bb = consts.tile([P, BLOCKS, DB], F32, name="rf_to_bb")
+        def turn_biases():
+            nc.vector.tensor_copy(out=bias_rows_f32[:], in_=bias_rows[:])
+            bank = rest.tile([P, CHUNK], F32, name="bank")
+            nc.tensor.transpose(bank[:, 0:P], bias_rows_f32[:], ident[:])
+            nc.vector.tensor_copy(out=bias[:], in_=bank[:, 0 : 2 * BLOCKS])
+            nc.vector.tensor_scalar_mul(out=neg_bias[:], in0=bias[:], scalar1=-1.0)
+            nc.vector.tensor_scalar(
+                out=steep_bias[:], in0=bias[:], scalar1=-4.0, scalar2=2.0 * math.log(2.0),
+                op0=ALU.mult, op1=ALU.add,
+            )
 
         def new_operand(label, passes):
             codes = keep.tile([P, passes, CHUNK], U32, name="codes_" + label, align_bytes=64)
             scales = keep.tile([P, passes, CHUNK], U8, name="scales_" + label, align_bytes=64)
             return {"codes": codes, "scales": scales, "passes": passes}
 
-        def regroup(rows, scalar_helps):
-            raw = raws.tile([P, BLOCKS, K_PASS], BF16, name="raw")
-            nc.sync.dma_start(out=raw[:], in_=rows)
-            words = raw[:].bitcast(F32)
-            grouped = groupeds.tile([P, CHUNK * PACK], BF16, name="grouped", align_bytes=64)
-            grouped_words = grouped[:].bitcast(F32).rearrange(
-                "p (j r u) -> p j r u", j=BLOCKS, u=2
-            )
-            for h in range(HALF):
-                bank = rest.tile([P, CHUNK], F32, name="bank")
-                flipped = bank[:].rearrange("p (j u r) -> p j u r", j=2, u=2)
-                for j in range(2):
-                    for u in range(2):
-                        nc.tensor.transpose(
-                            flipped[:, j, u, :],
-                            words[:, 2 * h + j, u : 2 * P : 2],
-                            ident[:],
-                        )
-                copy = nc.scalar.copy if scalar_helps and h == 1 else nc.vector.tensor_copy
-                copy(
-                    out=grouped_words[:, 2 * h : 2 * h + 2, :, :],
-                    in_=flipped.rearrange("p j u r -> p j r u"),
-                )
-            return grouped
+        w_bb = new_operand("w_bb", 1)
+        w_rf = new_operand("w_rf", DR // K_PASS)
+        x_rf = new_operand("x_rf", DR // K_PASS)
+        w_rf_rows = W_rfbb.rearrange("(j p) k -> p j k", p=P)
+        x_rf_rows = RF_feature.rearrange("(j p) k -> p j k", p=P)
 
-        def quantise(operand, c, grouped):
-            nc.vector.quantize_mx(
-                out=operand["codes"][:, c, :].bitcast(FP8X4),
-                scales=operand["scales"][:, c, :],
-                in_=grouped[:],
+        rf_chunk = {"x": x_rf, "w": w_rf, "bias": BLOCKS, "sample_block": None}
+        rf_passes = []
+        for c in range(DR // K_PASS):
+            k_cols = slice(c * K_PASS, (c + 1) * K_PASS)
+            rf_passes.append((w_rf, c, w_rf_rows[:, :, k_cols]))
+            rf_passes.append((x_rf, c, x_rf_rows[:, :, k_cols]))
+
+        bb_chunks = []
+        bb_passes = []
+        for n in range(B * G // CHUNK):
+            s, g0 = n // (G // BLOCKS), BLOCKS * (n % (G // BLOCKS))
+            x = new_operand("x_bb%d" % n, 1)
+            bb_chunks.append(
+                {"x": x, "w": w_bb, "bias": 0, "sample_block": s, "first_group": g0}
             )
+            bb_passes.append((x, 0, BB_feature[s * P : (s + 1) * P, g0 : g0 + BLOCKS, :]))
+
+        n_first = GROUP_SIZES[0]
+        groups = [bb_chunks[:n_first], bb_chunks[n_first:]]
+        assert len(groups[1]) == GROUP_SIZES[1]
+
+        passes = [(w_bb, 0, W_bbbb.rearrange("(j p) k -> p j k", p=P))]
+        passes = passes + bb_passes[:n_first] + rf_passes + bb_passes[n_first:]
 
         def product(bank, chunk, o):
             w, x = chunk["w"], chunk["x"]
@@ -125,19 +133,23 @@ def tile_gnn_layer_pb_t_kernel(
                 )
 
         def sigmoid(chunk):
-            act = acts.tile([P, BLOCKS, CHUNK], F32, name="act")
+            if chunk is rf_chunk:
+                act = consts.tile([P, BLOCKS, CHUNK], F32, name="rf_act")
+            else:
+                act = acts.tile([P, BLOCKS, CHUNK], F32, name="act")
             chunk["act"] = act
             for o in range(BLOCKS):
                 bank = front.tile([P, CHUNK], F32, name="first")
                 product(bank, chunk, o)
-                col = chunk["bias"] + o
+                col = slice(chunk["bias"] + o, chunk["bias"] + o + 1)
                 nc.scalar.activation(
-                    out=act[:, o, :],
-                    in_=bank[:],
-                    func=ACT.Sigmoid,
-                    bias=neg_bias[:, col : col + 1],
-                    scale=-1.0,
+                    out=act[:, o, :], in_=bank[:], func=ACT.Sigmoid, bias=neg_bias[:, col], scale=-1.0
                 )
+                if chunk is rf_chunk:
+                    nc.scalar.activation(
+                        out=steep[:, o, :], in_=bank[:], func=ACT.Sigmoid,
+                        bias=steep_bias[:, col], scale=-4.0,
+                    )
 
         def log(chunk):
             act = chunk["act"]
@@ -151,6 +163,19 @@ def tile_gnn_layer_pb_t_kernel(
                 half = act[:, 2 * h : 2 * h + 2, :]
                 nc.scalar.activation(out=half, in_=half, func=ACT.Tanh, scale=-1.0)
 
+        def tanh_without_log(spare):
+            fused = nc.vector.scalar_tensor_tensor
+            for h in range(HALF):
+                part = slice(2 * h, 2 * h + 2)
+                s, d, v = rf_chunk["act"][:, part, :], steep[:, part, :], spare[:, part, :]
+                fused(out=v, in0=s, scalar=-0.8, in1=s, op0=ALU.add, op1=ALU.mult)
+                fused(out=d, in0=v, scalar=0.2, in1=d, op0=ALU.add, op1=ALU.mult)
+                fused(out=v, in0=d, scalar=-1.25, in1=v, op0=ALU.mult, op1=ALU.add)
+                fused(out=s, in0=s, scalar=0.8, in1=v, op0=ALU.mult, op1=ALU.add)
+                nc.vector.tensor_scalar(
+                    out=s, in0=s, scalar1=-2.0, scalar2=1.0, op0=ALU.mult, op1=ALU.add
+                )
+
         def times_z(chunk, h):
             act = chunk["act"]
             for o in range(2 * h, 2 * h + 2):
@@ -158,122 +183,178 @@ def tile_gnn_layer_pb_t_kernel(
                 product(bank, chunk, o)
                 col = chunk["bias"] + o
                 nc.vector.scalar_tensor_tensor(
-                    out=act[:, o, :],
-                    in0=bank[:],
-                    scalar=bias[:, col : col + 1],
-                    in1=act[:, o, :],
-                    op0=ALU.add,
-                    op1=ALU.mult,
+                    out=act[:, o, :], in0=bank[:], scalar=bias[:, col : col + 1],
+                    in1=act[:, o, :], op0=ALU.add, op1=ALU.mult,
                 )
 
-        def turn_back(chunk, h):
-            act = chunk["act"]
-            for j in range(2 * h, 2 * h + 2):
+        def keep_z(chunk, z):
+            chunk["z"] = z
+            for o in range(BLOCKS):
                 bank = rest.tile([P, CHUNK], F32, name="bank")
-                for o in range(BLOCKS):
-                    nc.tensor.transpose(
-                        bank[:, o * P : (o + 1) * P], act[:, o, j * P : (j + 1) * P], ident[:]
-                    )
-                if chunk["sample_block"] is None:
-                    nc.vector.tensor_copy(out=rf_to_bb[:, j, :], in_=bank[:])
-                else:
-                    s = chunk["sample_block"]
-                    stage = stages.tile([P, DB], F32, name="stage")
-                    nc.vector.tensor_tensor(
-                        out=stage[:], in0=bank[:], in1=rf_to_bb[:, s, :], op=ALU.add
-                    )
-                    nc.sync.dma_start(
-                        out=out[s * P : (s + 1) * P, chunk["first_group"] + j, :], in_=stage[:]
-                    )
+                product(bank, chunk, o)
+                nc.vector.tensor_scalar_add(
+                    out=z[:, o, :], in0=bank[:], scalar1=bias[:, o : o + 1]
+                )
 
-        w_bb = new_operand("w_bb", 1)
-        w_rf = new_operand("w_rf", DR // K_PASS)
-        x_rf = new_operand("x_rf", DR // K_PASS)
-        w_bb_rows = W_bbbb.rearrange("(j p) k -> p j k", p=P)
-        w_rf_rows = W_rfbb.rearrange("(j p) k -> p j k", p=P)
-        x_rf_rows = RF_feature.rearrange("(j p) k -> p j k", p=P)
+        def times_kept_z(chunk):
+            for o in range(BLOCKS):
+                a = chunk["act"][:, o, :]
+                nc.gpsimd.tensor_tensor(out=a, in0=a, in1=chunk["z"][:, o, :], op=ALU.mult)
 
-        rf_chunk = {"x": x_rf, "w": w_rf, "bias": BLOCKS, "sample_block": None}
-        rf_passes = []
-        for c in range(DR // K_PASS):
-            k_cols = slice(c * K_PASS, (c + 1) * K_PASS)
-            rf_passes.append((w_rf, c, w_rf_rows[:, :, k_cols]))
-            rf_passes.append((x_rf, c, x_rf_rows[:, :, k_cols]))
-
-        bb_chunks = []
-        for n in range(B * G // CHUNK):
-            s, g0 = n // (G // BLOCKS), BLOCKS * (n % (G // BLOCKS))
-            bb_chunks.append(
-                {
-                    "x": new_operand("x_bb%d" % n, 1),
-                    "w": w_bb,
-                    "bias": 0,
-                    "sample_block": s,
-                    "first_group": g0,
-                }
+        def turn_back(chunk, j, on_scalar):
+            act, s = chunk["act"], chunk["sample_block"]
+            bank = rest.tile([P, CHUNK], F32, name="bank")
+            for o in range(BLOCKS):
+                cols = slice(o * P, (o + 1) * P)
+                nc.tensor.matmul(
+                    bank[:, cols], lhsT=act[:, o, j * P : (j + 1) * P], rhs=ident[:],
+                    is_transpose=True, start=True, stop=not on_scalar,
+                )
+                if on_scalar:
+                    nc.tensor.matmul(
+                        bank[:, cols], lhsT=rf_chunk["act"][:, o, s * P : (s + 1) * P],
+                        rhs=ident[:], is_transpose=True, start=False, stop=True,
+                    )
+            if chunk is rf_chunk:
+                nc.vector.tensor_copy(out=rf_to_bb[:, j, :], in_=bank[:])
+                return
+            stage = stages.tile([P, DB], F32, name="stage")
+            if on_scalar:
+                nc.scalar.copy(out=stage[:], in_=bank[:])
+            else:
+                nc.vector.tensor_tensor(
+                    out=stage[:], in0=bank[:], in1=rf_to_bb[:, s, :], op=ALU.add
+                )
+            nc.sync.dma_start(
+                out=out[s * P : (s + 1) * P, chunk["first_group"] + j, :], in_=stage[:]
             )
 
-        def bb_pass(chunk):
-            s, g0 = chunk["sample_block"], chunk["first_group"]
-            return (chunk["x"], 0, BB_feature[s * P : (s + 1) * P, g0 : g0 + BLOCKS, :])
+        with ExitStack() as preparing:
+            raws = preparing.enter_context(tc.tile_pool(name="raws", bufs=4))
+            groupeds = preparing.enter_context(tc.tile_pool(name="groupeds", bufs=4))
 
-        n_first = GROUP_SIZES[0] - 1
-        groups = [[rf_chunk] + bb_chunks[:n_first]]
-        start = n_first
-        for size in GROUP_SIZES[1:]:
-            groups.append(bb_chunks[start : start + size])
-            start += size
-        assert start == len(bb_chunks)
+            def start_pass(k):
+                raw = raws.tile([P, BLOCKS, K_PASS], BF16, name="raw")
+                grouped = groupeds.tile([P, CHUNK * PACK], BF16, name="grouped", align_bytes=64)
+                return {"k": k, "raw": raw, "grouped": grouped}
 
-        passes = [(w_bb, 0, w_bb_rows)]
-        passes.extend([bb_pass(chunk) for chunk in bb_chunks[:n_first]])
-        passes.extend(rf_passes)
-        passes.extend([bb_pass(chunk) for chunk in bb_chunks[n_first:]])
+            def load(item, blocks):
+                nc.sync.dma_start(out=item["raw"][:, blocks, :], in_=passes[item["k"]][2][:, blocks, :])
 
-        def written_before(i):
-            return min(len(passes), LEAD + i + i // 3)
+            def regroup(item, j0, n, pool, name, copy):
+                words = item["raw"][:].bitcast(F32)
+                grouped_words = item["grouped"][:].bitcast(F32).rearrange(
+                    "p (j r u) -> p j r u", j=BLOCKS, u=2
+                )
+                bank = pool.tile([P, CHUNK], F32, name=name)
+                flipped = bank[:, 0 : n * 2 * P].rearrange("p (j u r) -> p j u r", j=n, u=2)
+                for j in range(n):
+                    for u in range(2):
+                        nc.tensor.transpose(
+                            flipped[:, j, u, :], words[:, j0 + j, u : 2 * P : 2], ident[:]
+                        )
+                copy(
+                    out=grouped_words[:, j0 : j0 + n, :, :],
+                    in_=flipped.rearrange("p j u r -> p j r u"),
+                )
 
-        state = {"pending": None}
+            def quantise(item, j0, n):
+                operand, c = passes[item["k"]][0], passes[item["k"]][1]
+                cols = slice(j0 * P, (j0 + n) * P)
+                nc.vector.quantize_mx(
+                    out=operand["codes"][:, c, cols].bitcast(FP8X4),
+                    scales=operand["scales"][:, c, cols],
+                    in_=item["grouped"][:, j0 * K_PASS : (j0 + n) * K_PASS],
+                )
 
-        def quantise_pending():
-            if state["pending"] is not None:
-                quantise(*state["pending"])
-                state["pending"] = None
+            vector_copy, scalar_copy = nc.vector.tensor_copy, nc.scalar.copy
+            first_w, first_x = start_pass(0), start_pass(1)
+            load(first_w, slice(0, 1))
+            for j in range(BLOCKS):
+                load(first_x, slice(j, j + 1))
+            load_biases()
+            for j in range(1, BLOCKS):
+                load(first_w, slice(j, j + 1))
+            regroup(first_w, 0, 1, rest, "bank", vector_copy)
+            regroup(first_x, 0, 1, rest, "bank", scalar_copy)
+            regroup(first_x, 1, 1, rest, "bank", vector_copy)
+            quantise(first_w, 0, 1)
+            regroup(first_x, 2, 1, rest, "bank", scalar_copy)
+            regroup(first_x, 3, 1, rest, "bank", vector_copy)
+            turn_biases()
+            quantise(first_x, 0, BLOCKS)
+            regroup(first_w, 1, 1, front, "first", vector_copy)
+            for j in range(2, BLOCKS):
+                regroup(first_w, j, 1, front, "first", vector_copy)
+                quantise(first_w, j - 1, 1)
+            quantise(first_w, BLOCKS - 1, 1)
+            sigmoid(groups[0][0])
 
-        def prepare(k, scalar_helps=False):
-            operand, c, rows = passes[k]
-            grouped = regroup(rows, scalar_helps)
+            state = {"pending": None, "done": 2}
+
+            def quantise_pending():
+                if state["pending"] is not None:
+                    quantise(state["pending"], 0, BLOCKS)
+
+            def prepare_up_to(n, scalar_helps):
+                while state["done"] < min(n, len(passes)):
+                    item = start_pass(state["done"])
+                    load(item, slice(0, BLOCKS))
+                    for h in range(HALF):
+                        copy = scalar_copy if scalar_helps and h == 1 else vector_copy
+                        regroup(item, 2 * h, 2, rest, "bank", copy)
+                    quantise_pending()
+                    state["pending"] = item
+                    state["done"] += 1
+
+            prepare_up_to(LEAD, True)
+            for i, chunk in enumerate(groups[0] + [rf_chunk]):
+                prepare_up_to(LEAD + i + i // 3, False)
+                if i > 0:
+                    sigmoid(chunk)
+            assert state["done"] > 1 + n_first + len(rf_passes)
+            prepare_up_to(len(passes), False)
             quantise_pending()
-            state["pending"] = (operand, c, grouped)
 
-        prepare(0, scalar_helps=True)
-        prepare(1, scalar_helps=True)
-        quantise_pending()
-        done = 2
-        for i, chunk in enumerate(bb_chunks[:n_first] + [rf_chunk]):
-            for k in range(done, written_before(i)):
-                prepare(k)
-            done = written_before(i)
-            sigmoid(chunk)
-        assert done > 1 + n_first + len(rf_passes)
-        for k in range(done, len(passes)):
-            prepare(k)
-        quantise_pending()
-
+        zs = ctx.enter_context(tc.tile_pool(name="zs", bufs=4))
         for g, group in enumerate(groups):
             following = groups[g + 1] if g + 1 < len(groups) else []
             for chunk in group:
                 log(chunk)
-            call_in_sigmoid_table()
-            previous = None
-            for i, chunk in enumerate(group):
-                tanh(chunk)
-                if i < len(following):
-                    sigmoid(following[i])
+
+            if g == 0:
+                spare = zs.tile([P, BLOCKS, CHUNK], F32, name="z")
+                tanh_without_log(spare)
                 for h in range(HALF):
-                    times_z(chunk, h)
-                    if previous is not None:
-                        turn_back(previous, h)
-                previous = chunk
-            for h in range(HALF):
-                turn_back(previous, h)
+                    times_z(rf_chunk, h)
+                for j in range(BLOCKS):
+                    turn_back(rf_chunk, j, False)
+            for i in KEPT[g]:
+                z = zs.tile([P, BLOCKS, CHUNK], F32, name="z")
+                keep_z(group[i], z)
+
+            call_in_sigmoid_table()
+            due = {}
+            for i in range(len(group) + 1):
+                turns = []
+                for step in sorted(due):
+                    if step == i or step > i == len(group):
+                        turns.extend([(c, j) for c in due[step] for j in range(BLOCKS)])
+                times = []
+                if i < len(group):
+                    chunk = group[i]
+                    tanh(chunk)
+                    if i >= 2 and i % 2 == 0 and i // 2 - 1 < len(following):
+                        sigmoid(following[i // 2 - 1])
+                    if i in KEPT[g]:
+                        times_kept_z(chunk)
+                        due.setdefault(i + KEPT_DELAY, []).append(chunk)
+                    else:
+                        times = [chunk]
+                        due.setdefault(i + 1, []).append(chunk)
+                shared = not following and i >= len(group) - 1
+                for h in range(HALF):
+                    for c in times:
+                        times_z(c, h)
+                    for c, j in turns[h * len(turns) // 2 : (h + 1) * len(turns) // 2]:
+                        turn_back(c, j, shared and j % 2 == 1)

@@ -22,10 +22,7 @@ BLOCKS = 4
 CHUNK = BLOCKS * P
 HALF = BLOCKS // 2
 
-GROUP_SIZES = (12, 4)
-
-KEPT = ((0, 3, 6, 9), (1,))
-KEPT_DELAY = 3
+GROUP_SIZES = (9, 5, 2)
 
 LEAD = 4
 
@@ -39,7 +36,7 @@ def tile_gnn_layer_pb_t_kernel(
     with ExitStack() as ctx:
         consts = ctx.enter_context(tc.tile_pool(name="consts", bufs=1))
         keep = ctx.enter_context(tc.tile_pool(name="keep", bufs=1))
-        acts = ctx.enter_context(tc.tile_pool(name="acts", bufs=13))
+        acts = ctx.enter_context(tc.tile_pool(name="acts", bufs=12))
         stages = ctx.enter_context(tc.tile_pool(name="stages", bufs=8))
         front = ctx.enter_context(tc.psum_pool(name="front", bufs=4))
         rest = ctx.enter_context(tc.psum_pool(name="rest", bufs=4))
@@ -57,6 +54,7 @@ def tile_gnn_layer_pb_t_kernel(
         steep_bias = consts.tile([P, 2 * BLOCKS], F32, name="steep_bias")
         rf_to_bb = consts.tile([P, BLOCKS, DB], F32, name="rf_to_bb")
         steep = consts.tile([P, BLOCKS, CHUNK], F32, name="steep")
+        spare = consts.tile([P, BLOCKS, CHUNK], F32, name="spare")
         scratch = consts.tile([P, 1], F32, name="scratch")
 
         def call_in_sigmoid_table():
@@ -111,9 +109,12 @@ def tile_gnn_layer_pb_t_kernel(
             )
             bb_passes.append((x, 0, BB_feature[s * P : (s + 1) * P, g0 : g0 + BLOCKS, :]))
 
+        groups, start = [], 0
+        for size in GROUP_SIZES:
+            groups.append(bb_chunks[start : start + size])
+            start += size
+        assert start == len(bb_chunks)
         n_first = GROUP_SIZES[0]
-        groups = [bb_chunks[:n_first], bb_chunks[n_first:]]
-        assert len(groups[1]) == GROUP_SIZES[1]
 
         passes = [(w_bb, 0, W_bbbb.rearrange("(j p) k -> p j k", p=P))]
         passes = passes + bb_passes[:n_first] + rf_passes + bb_passes[n_first:]
@@ -163,7 +164,7 @@ def tile_gnn_layer_pb_t_kernel(
                 half = act[:, 2 * h : 2 * h + 2, :]
                 nc.scalar.activation(out=half, in_=half, func=ACT.Tanh, scale=-1.0)
 
-        def tanh_without_log(spare):
+        def tanh_without_log():
             fused = nc.vector.scalar_tensor_tensor
             for h in range(HALF):
                 part = slice(2 * h, 2 * h + 2)
@@ -186,20 +187,6 @@ def tile_gnn_layer_pb_t_kernel(
                     out=act[:, o, :], in0=bank[:], scalar=bias[:, col : col + 1],
                     in1=act[:, o, :], op0=ALU.add, op1=ALU.mult,
                 )
-
-        def keep_z(chunk, z):
-            chunk["z"] = z
-            for o in range(BLOCKS):
-                bank = rest.tile([P, CHUNK], F32, name="bank")
-                product(bank, chunk, o)
-                nc.vector.tensor_scalar_add(
-                    out=z[:, o, :], in0=bank[:], scalar1=bias[:, o : o + 1]
-                )
-
-        def times_kept_z(chunk):
-            for o in range(BLOCKS):
-                a = chunk["act"][:, o, :]
-                nc.gpsimd.tensor_tensor(out=a, in0=a, in1=chunk["z"][:, o, :], op=ALU.mult)
 
         def turn_back(chunk, j, on_scalar):
             act, s = chunk["act"], chunk["sample_block"]
@@ -295,6 +282,7 @@ def tile_gnn_layer_pb_t_kernel(
             def quantise_pending():
                 if state["pending"] is not None:
                     quantise(state["pending"], 0, BLOCKS)
+                    state["pending"] = None
 
             def prepare_up_to(n, scalar_helps):
                 while state["done"] < min(n, len(passes)):
@@ -307,54 +295,39 @@ def tile_gnn_layer_pb_t_kernel(
                     state["pending"] = item
                     state["done"] += 1
 
+            n_needed = 1 + n_first + len(rf_passes)
             prepare_up_to(LEAD, True)
             for i, chunk in enumerate(groups[0] + [rf_chunk]):
-                prepare_up_to(LEAD + i + i // 3, False)
+                prepare_up_to(min(n_needed, LEAD + i + i // 3), False)
+                if state["done"] == n_needed:
+                    quantise_pending()
                 if i > 0:
                     sigmoid(chunk)
-            assert state["done"] > 1 + n_first + len(rf_passes)
             prepare_up_to(len(passes), False)
             quantise_pending()
 
-        zs = ctx.enter_context(tc.tile_pool(name="zs", bufs=4))
         for g, group in enumerate(groups):
             following = groups[g + 1] if g + 1 < len(groups) else []
             for chunk in group:
                 log(chunk)
-
             if g == 0:
-                spare = zs.tile([P, BLOCKS, CHUNK], F32, name="z")
-                tanh_without_log(spare)
+                tanh_without_log()
                 for h in range(HALF):
                     times_z(rf_chunk, h)
                 for j in range(BLOCKS):
                     turn_back(rf_chunk, j, False)
-            for i in KEPT[g]:
-                z = zs.tile([P, BLOCKS, CHUNK], F32, name="z")
-                keep_z(group[i], z)
-
             call_in_sigmoid_table()
-            due = {}
+            previous = None
             for i in range(len(group) + 1):
-                turns = []
-                for step in sorted(due):
-                    if step == i or step > i == len(group):
-                        turns.extend([(c, j) for c in due[step] for j in range(BLOCKS)])
-                times = []
                 if i < len(group):
-                    chunk = group[i]
-                    tanh(chunk)
-                    if i >= 2 and i % 2 == 0 and i // 2 - 1 < len(following):
-                        sigmoid(following[i // 2 - 1])
-                    if i in KEPT[g]:
-                        times_kept_z(chunk)
-                        due.setdefault(i + KEPT_DELAY, []).append(chunk)
-                    else:
-                        times = [chunk]
-                        due.setdefault(i + 1, []).append(chunk)
+                    tanh(group[i])
+                if i < min(len(group), len(following)):
+                    sigmoid(following[i])
                 shared = not following and i >= len(group) - 1
                 for h in range(HALF):
-                    for c in times:
-                        times_z(c, h)
-                    for c, j in turns[h * len(turns) // 2 : (h + 1) * len(turns) // 2]:
-                        turn_back(c, j, shared and j % 2 == 1)
+                    if i < len(group):
+                        times_z(group[i], h)
+                    if previous is not None:
+                        turn_back(previous, 2 * h, False)
+                        turn_back(previous, 2 * h + 1, shared)
+                previous = group[i] if i < len(group) else None

@@ -166,13 +166,19 @@ def tile_gnn_layer_pb_t_kernel(
 
         def tanh_without_log():
             fused = nc.vector.scalar_tensor_tensor
+            parts = []
             for h in range(HALF):
                 part = slice(2 * h, 2 * h + 2)
-                s, d, v = rf_chunk["act"][:, part, :], steep[:, part, :], spare[:, part, :]
+                parts.append((rf_chunk["act"][:, part, :], steep[:, part, :], spare[:, part, :]))
+            for s, d, v in parts:
                 fused(out=v, in0=s, scalar=-0.8, in1=s, op0=ALU.add, op1=ALU.mult)
+            for s, d, v in parts:
                 fused(out=d, in0=v, scalar=0.2, in1=d, op0=ALU.add, op1=ALU.mult)
+            for s, d, v in parts:
                 fused(out=v, in0=d, scalar=-1.25, in1=v, op0=ALU.mult, op1=ALU.add)
+            for s, d, v in parts:
                 fused(out=s, in0=s, scalar=0.8, in1=v, op0=ALU.mult, op1=ALU.add)
+            for s, d, v in parts:
                 nc.vector.tensor_scalar(
                     out=s, in0=s, scalar1=-2.0, scalar2=1.0, op0=ALU.mult, op1=ALU.add
                 )
@@ -314,8 +320,6 @@ def tile_gnn_layer_pb_t_kernel(
                 tanh_without_log()
                 for h in range(HALF):
                     times_z(rf_chunk, h)
-                for j in range(BLOCKS):
-                    turn_back(rf_chunk, j, False)
             call_in_sigmoid_table()
             previous = None
             for i in range(len(group) + 1):
@@ -323,6 +327,9 @@ def tile_gnn_layer_pb_t_kernel(
                     tanh(group[i])
                 if i < min(len(group), len(following)):
                     sigmoid(following[i])
+                if g == 0 and i == 0:
+                    for j in range(BLOCKS):
+                        turn_back(rf_chunk, j, False)
                 shared = not following and i >= len(group) - 1
                 for h in range(HALF):
                     if i < len(group):

@@ -23,6 +23,7 @@ CHUNK = BLOCKS * P
 HALF = BLOCKS // 2
 
 GROUP_SIZES = (9, 5, 2)
+QUICK = 9
 
 LEAD = 4
 
@@ -115,6 +116,8 @@ def tile_gnn_layer_pb_t_kernel(
             start += size
         assert start == len(bb_chunks)
         n_first = GROUP_SIZES[0]
+        quick = bb_chunks[QUICK]
+        groups[1] = [c for c in groups[1] if c["x"] is not quick["x"]]
 
         passes = [(w_bb, 0, W_bbbb.rearrange("(j p) k -> p j k", p=P))]
         passes = passes + bb_passes[:n_first] + rf_passes + bb_passes[n_first:]
@@ -146,7 +149,7 @@ def tile_gnn_layer_pb_t_kernel(
                 nc.scalar.activation(
                     out=act[:, o, :], in_=bank[:], func=ACT.Sigmoid, bias=neg_bias[:, col], scale=-1.0
                 )
-                if chunk is rf_chunk:
+                if chunk is rf_chunk or chunk is quick:
                     nc.scalar.activation(
                         out=steep[:, o, :], in_=bank[:], func=ACT.Sigmoid,
                         bias=steep_bias[:, col], scale=-4.0,
@@ -164,12 +167,12 @@ def tile_gnn_layer_pb_t_kernel(
                 half = act[:, 2 * h : 2 * h + 2, :]
                 nc.scalar.activation(out=half, in_=half, func=ACT.Tanh, scale=-1.0)
 
-        def tanh_without_log():
+        def tanh_without_log(chunk):
             fused = nc.vector.scalar_tensor_tensor
             parts = []
             for h in range(HALF):
                 part = slice(2 * h, 2 * h + 2)
-                parts.append((rf_chunk["act"][:, part, :], steep[:, part, :], spare[:, part, :]))
+                parts.append((chunk["act"][:, part, :], steep[:, part, :], spare[:, part, :]))
             for s, d, v in parts:
                 fused(out=v, in0=s, scalar=-0.8, in1=s, op0=ALU.add, op1=ALU.mult)
             for s, d, v in parts:
@@ -182,6 +185,23 @@ def tile_gnn_layer_pb_t_kernel(
                 nc.vector.tensor_scalar(
                     out=s, in0=s, scalar1=-2.0, scalar2=1.0, op0=ALU.mult, op1=ALU.add
                 )
+
+        def tanh_on_gpsimd(chunk):
+            for o in range(BLOCKS):
+                s, d, v = chunk["act"][:, o, :], steep[:, o, :], spare[:, o, :]
+                nc.gpsimd.tensor_tensor(out=v, in0=s, in1=s, op=ALU.mult)
+                nc.gpsimd.tensor_scalar(
+                    out=s, in0=s, scalar1=-0.8, scalar2=0.2, op0=ALU.mult, op1=ALU.add
+                )
+                nc.gpsimd.tensor_tensor(out=s, in0=s, in1=v, op=ALU.add)
+                nc.gpsimd.tensor_tensor(out=d, in0=d, in1=s, op=ALU.mult)
+                nc.gpsimd.tensor_scalar(
+                    out=v, in0=v, scalar1=-2.0, scalar2=1.0, op0=ALU.mult, op1=ALU.add
+                )
+                nc.gpsimd.tensor_scalar(
+                    out=d, in0=d, scalar1=2.5, scalar2=0.0, op0=ALU.mult, op1=ALU.add
+                )
+                nc.gpsimd.tensor_tensor(out=s, in0=v, in1=d, op=ALU.add)
 
         def times_z(chunk, h):
             act = chunk["act"]
@@ -262,19 +282,19 @@ def tile_gnn_layer_pb_t_kernel(
 
             vector_copy, scalar_copy = nc.vector.tensor_copy, nc.scalar.copy
             first_w, first_x = start_pass(0), start_pass(1)
+            load_biases()
             load(first_w, slice(0, 1))
             for j in range(BLOCKS):
                 load(first_x, slice(j, j + 1))
-            load_biases()
             for j in range(1, BLOCKS):
                 load(first_w, slice(j, j + 1))
+            turn_biases()
             regroup(first_w, 0, 1, rest, "bank", vector_copy)
             regroup(first_x, 0, 1, rest, "bank", scalar_copy)
             regroup(first_x, 1, 1, rest, "bank", vector_copy)
             quantise(first_w, 0, 1)
             regroup(first_x, 2, 1, rest, "bank", scalar_copy)
             regroup(first_x, 3, 1, rest, "bank", vector_copy)
-            turn_biases()
             quantise(first_x, 0, BLOCKS)
             regroup(first_w, 1, 1, front, "first", vector_copy)
             for j in range(2, BLOCKS):
@@ -314,19 +334,27 @@ def tile_gnn_layer_pb_t_kernel(
 
         for g, group in enumerate(groups):
             following = groups[g + 1] if g + 1 < len(groups) else []
+            if g == 0:
+                following = [quick] + following
             for chunk in group:
                 log(chunk)
             if g == 0:
-                tanh_without_log()
+                tanh_without_log(rf_chunk)
                 for h in range(HALF):
                     times_z(rf_chunk, h)
             call_in_sigmoid_table()
             previous = None
+            if g == 1:
+                for h in range(HALF):
+                    times_z(quick, h)
+                previous = quick
             for i in range(len(group) + 1):
                 if i < len(group):
                     tanh(group[i])
                 if i < min(len(group), len(following)):
                     sigmoid(following[i])
+                    if following[i] is quick:
+                        tanh_on_gpsimd(quick)
                 if g == 0 and i == 0:
                     for j in range(BLOCKS):
                         turn_back(rf_chunk, j, False)

@@ -22,8 +22,7 @@ BLOCKS = 4
 CHUNK = BLOCKS * P
 HALF = BLOCKS // 2
 
-GROUP_SIZES = (9, 5, 2)
-QUICK = 9
+GROUP_SIZES = (8, 4, 2)
 
 LEAD = 4
 
@@ -38,7 +37,6 @@ def tile_gnn_layer_pb_t_kernel(
         consts = ctx.enter_context(tc.tile_pool(name="consts", bufs=1))
         keep = ctx.enter_context(tc.tile_pool(name="keep", bufs=1))
         acts = ctx.enter_context(tc.tile_pool(name="acts", bufs=12))
-        stages = ctx.enter_context(tc.tile_pool(name="stages", bufs=8))
         front = ctx.enter_context(tc.psum_pool(name="front", bufs=4))
         rest = ctx.enter_context(tc.psum_pool(name="rest", bufs=4))
         ctx.enter_context(tc.manual_schedule())
@@ -56,6 +54,8 @@ def tile_gnn_layer_pb_t_kernel(
         rf_to_bb = consts.tile([P, BLOCKS, DB], F32, name="rf_to_bb")
         steep = consts.tile([P, BLOCKS, CHUNK], F32, name="steep")
         spare = consts.tile([P, BLOCKS, CHUNK], F32, name="spare")
+        steep_quick = consts.tile([P, BLOCKS, CHUNK], F32, name="steep_quick")
+        spare_quick = consts.tile([P, BLOCKS, CHUNK], F32, name="spare_quick")
         scratch = consts.tile([P, 1], F32, name="scratch")
 
         def call_in_sigmoid_table():
@@ -110,14 +110,18 @@ def tile_gnn_layer_pb_t_kernel(
             )
             bb_passes.append((x, 0, BB_feature[s * P : (s + 1) * P, g0 : g0 + BLOCKS, :]))
 
-        groups, start = [], 0
-        for size in GROUP_SIZES:
+        quick, groups, start = [], [], 0
+        for g, size in enumerate(GROUP_SIZES):
+            if g < 2:
+                quick.append(bb_chunks[start])
+                start += 1
             groups.append(bb_chunks[start : start + size])
             start += size
         assert start == len(bb_chunks)
-        n_first = GROUP_SIZES[0]
-        quick = bb_chunks[QUICK]
-        groups[1] = [c for c in groups[1] if c["x"] is not quick["x"]]
+        n_first = 1 + GROUP_SIZES[0]
+        for chunk in [rf_chunk] + quick:
+            chunk["steep"], chunk["spare"] = steep, spare
+        quick[0]["steep"], quick[0]["spare"] = steep_quick, spare_quick
 
         passes = [(w_bb, 0, W_bbbb.rearrange("(j p) k -> p j k", p=P))]
         passes = passes + bb_passes[:n_first] + rf_passes + bb_passes[n_first:]
@@ -149,9 +153,9 @@ def tile_gnn_layer_pb_t_kernel(
                 nc.scalar.activation(
                     out=act[:, o, :], in_=bank[:], func=ACT.Sigmoid, bias=neg_bias[:, col], scale=-1.0
                 )
-                if chunk is rf_chunk or chunk is quick:
+                if "steep" in chunk:
                     nc.scalar.activation(
-                        out=steep[:, o, :], in_=bank[:], func=ACT.Sigmoid,
+                        out=chunk["steep"][:, o, :], in_=bank[:], func=ACT.Sigmoid,
                         bias=steep_bias[:, col], scale=-4.0,
                     )
 
@@ -172,7 +176,9 @@ def tile_gnn_layer_pb_t_kernel(
             parts = []
             for h in range(HALF):
                 part = slice(2 * h, 2 * h + 2)
-                parts.append((chunk["act"][:, part, :], steep[:, part, :], spare[:, part, :]))
+                parts.append(
+                    (chunk["act"][:, part, :], chunk["steep"][:, part, :], chunk["spare"][:, part, :])
+                )
             for s, d, v in parts:
                 fused(out=v, in0=s, scalar=-0.8, in1=s, op0=ALU.add, op1=ALU.mult)
             for s, d, v in parts:
@@ -188,7 +194,7 @@ def tile_gnn_layer_pb_t_kernel(
 
         def tanh_on_gpsimd(chunk):
             for o in range(BLOCKS):
-                s, d, v = chunk["act"][:, o, :], steep[:, o, :], spare[:, o, :]
+                s, d, v = chunk["act"][:, o, :], chunk["steep"][:, o, :], chunk["spare"][:, o, :]
                 nc.gpsimd.tensor_tensor(out=v, in0=s, in1=s, op=ALU.mult)
                 nc.gpsimd.tensor_scalar(
                     out=s, in0=s, scalar1=-0.8, scalar2=0.2, op0=ALU.mult, op1=ALU.add
@@ -214,6 +220,8 @@ def tile_gnn_layer_pb_t_kernel(
                     in1=act[:, o, :], op0=ALU.add, op1=ALU.mult,
                 )
 
+        late = {}
+
         def turn_back(chunk, j, on_scalar):
             act, s = chunk["act"], chunk["sample_block"]
             bank = rest.tile([P, CHUNK], F32, name="bank")
@@ -231,7 +239,7 @@ def tile_gnn_layer_pb_t_kernel(
             if chunk is rf_chunk:
                 nc.vector.tensor_copy(out=rf_to_bb[:, j, :], in_=bank[:])
                 return
-            stage = stages.tile([P, DB], F32, name="stage")
+            stage = late["stages"].tile([P, DB], F32, name="stage")
             if on_scalar:
                 nc.scalar.copy(out=stage[:], in_=bank[:])
             else:
@@ -301,7 +309,8 @@ def tile_gnn_layer_pb_t_kernel(
                 regroup(first_w, j, 1, front, "first", vector_copy)
                 quantise(first_w, j - 1, 1)
             quantise(first_w, BLOCKS - 1, 1)
-            sigmoid(groups[0][0])
+            sigmoid(quick[0])
+            tanh_on_gpsimd(quick[0])
 
             state = {"pending": None, "done": 2}
 
@@ -310,32 +319,31 @@ def tile_gnn_layer_pb_t_kernel(
                     quantise(state["pending"], 0, BLOCKS)
                     state["pending"] = None
 
-            def prepare_up_to(n, scalar_helps):
+            def prepare_up_to(n):
                 while state["done"] < min(n, len(passes)):
                     item = start_pass(state["done"])
                     load(item, slice(0, BLOCKS))
                     for h in range(HALF):
-                        copy = scalar_copy if scalar_helps and h == 1 else vector_copy
-                        regroup(item, 2 * h, 2, rest, "bank", copy)
+                        regroup(item, 2 * h, 2, rest, "bank", vector_copy)
                     quantise_pending()
                     state["pending"] = item
                     state["done"] += 1
 
             n_needed = 1 + n_first + len(rf_passes)
-            prepare_up_to(LEAD, True)
-            for i, chunk in enumerate(groups[0] + [rf_chunk]):
-                prepare_up_to(min(n_needed, LEAD + i + i // 3), False)
+            for i, chunk in enumerate([quick[0]] + groups[0] + [rf_chunk]):
+                prepare_up_to(min(n_needed, LEAD + i + i // 3))
                 if state["done"] == n_needed:
                     quantise_pending()
                 if i > 0:
                     sigmoid(chunk)
-            prepare_up_to(len(passes), False)
+            prepare_up_to(len(passes))
             quantise_pending()
 
+        late["stages"] = ctx.enter_context(tc.tile_pool(name="stages", bufs=8))
         for g, group in enumerate(groups):
             following = groups[g + 1] if g + 1 < len(groups) else []
             if g == 0:
-                following = [quick] + following
+                following = [quick[1]] + following
             for chunk in group:
                 log(chunk)
             if g == 0:
@@ -344,17 +352,17 @@ def tile_gnn_layer_pb_t_kernel(
                     times_z(rf_chunk, h)
             call_in_sigmoid_table()
             previous = None
-            if g == 1:
+            if g < 2:
                 for h in range(HALF):
-                    times_z(quick, h)
-                previous = quick
+                    times_z(quick[g], h)
+                previous = quick[g]
             for i in range(len(group) + 1):
                 if i < len(group):
                     tanh(group[i])
                 if i < min(len(group), len(following)):
                     sigmoid(following[i])
-                    if following[i] is quick:
-                        tanh_on_gpsimd(quick)
+                    if following[i] is quick[1]:
+                        tanh_on_gpsimd(quick[1])
                 if g == 0 and i == 0:
                     for j in range(BLOCKS):
                         turn_back(rf_chunk, j, False)

import math
from contextlib import ExitStack

import concourse.mybir as mybir
from concourse.masks import make_identity

F32 = mybir.dt.float32
BF16 = mybir.dt.bfloat16
U32 = mybir.dt.uint32
U8 = mybir.dt.uint8
FP8X4 = mybir.dt.float8_e4m3fn_x4
ACT = mybir.ActivationFunctionType
ALU = mybir.AluOpType

B, G, DB, DR = 512, 16, 512, 1024
FLOPS = 2 * B * G * DB * DB + 2 * B * DR * DB

P = 128
PACK = 4
K_PASS = P * PACK
BLOCKS = 4
CHUNK = BLOCKS * P
HALF = BLOCKS // 2

GROUP_SIZES = (8, 4, 2)

LEAD = 4

GUARD = 2.0 ** -60


def tile_gnn_layer_pb_t_kernel(
    tc, BB_feature, RF_feature, W_bbbb, b_bbbb, W_rfbb, b_rfbb, out
):
    nc = tc.nc
    with ExitStack() as ctx:
        consts = ctx.enter_context(tc.tile_pool(name="consts", bufs=1))
        keep = ctx.enter_context(tc.tile_pool(name="keep", bufs=1))
        acts = ctx.enter_context(tc.tile_pool(name="acts", bufs=12))
        front = ctx.enter_context(tc.psum_pool(name="front", bufs=4))
        rest = ctx.enter_context(tc.psum_pool(name="rest", bufs=4))
        ctx.enter_context(tc.manual_schedule())

        ident = consts.tile([P, P], F32, name="ident")
        make_identity(nc, ident[:])
        guard = consts.tile([P, 1], F32, name="guard")
        nc.vector.memset(guard[:], GUARD)
        bias_rows = consts.tile([P, P], BF16, name="bias_rows")
        nc.vector.memset(bias_rows[:], 0.0)
        bias_rows_f32 = consts.tile([P, P], F32, name="bias_rows_f32")
        bias = consts.tile([P, 2 * BLOCKS], F32, name="bias")
        neg_bias = consts.tile([P, 2 * BLOCKS], F32, name="neg_bias")
        steep_bias = consts.tile([P, 2 * BLOCKS], F32, name="steep_bias")
        rf_to_bb = consts.tile([P, BLOCKS, DB], F32, name="rf_to_bb")
        steep = consts.tile([P, BLOCKS, CHUNK], F32, name="steep")
        spare = consts.tile([P, BLOCKS, CHUNK], F32, name="spare")
        steep_quick = consts.tile([P, BLOCKS, CHUNK], F32, name="steep_quick")
        spare_quick = consts.tile([P, BLOCKS, CHUNK], F32, name="spare_quick")
        scratch = consts.tile([P, 1], F32, name="scratch")

        def call_in_sigmoid_table():
            nc.scalar.activation(out=scratch[:], in_=guard[:], func=ACT.Sigmoid)

        call_in_sigmoid_table()

        def load_biases():
            nc.sync.dma_start(
                out=bias_rows[0:BLOCKS, :], in_=b_bbbb.rearrange("(o p) -> o p", p=P)
            )
            nc.sync.dma_start(
                out=bias_rows[BLOCKS : 2 * BLOCKS, :], in_=b_rfbb.rearrange("(o p) -> o p", p=P)
            )

        def turn_biases():
            nc.vector.tensor_copy(out=bias_rows_f32[:], in_=bias_rows[:])
            bank = rest.tile([P, CHUNK], F32, name="bank")
            nc.tensor.transpose(bank[:, 0:P], bias_rows_f32[:], ident[:])
            nc.vector.tensor_copy(out=bias[:], in_=bank[:, 0 : 2 * BLOCKS])
            nc.vector.tensor_scalar_mul(out=neg_bias[:], in0=bias[:], scalar1=-1.0)
            nc.vector.tensor_scalar(
                out=steep_bias[:], in0=bias[:], scalar1=-4.0, scalar2=2.0 * math.log(2.0),
                op0=ALU.mult, op1=ALU.add,
            )

        def new_operand(label, passes):
            codes = keep.tile([P, passes, CHUNK], U32, name="codes_" + label, align_bytes=64)
            scales = keep.tile([P, passes, CHUNK], U8, name="scales_" + label, align_bytes=64)
            return {"codes": codes, "scales": scales, "passes": passes}

        w_bb = new_operand("w_bb", 1)
        w_rf = new_operand("w_rf", DR // K_PASS)
        x_rf = new_operand("x_rf", DR // K_PASS)
        w_rf_rows = W_rfbb.rearrange("(j p) k -> p j k", p=P)
        x_rf_rows = RF_feature.rearrange("(j p) k -> p j k", p=P)

        rf_chunk = {"x": x_rf, "w": w_rf, "bias": BLOCKS, "sample_block": None}
        rf_passes = []
        for c in range(DR // K_PASS):
            k_cols = slice(c * K_PASS, (c + 1) * K_PASS)
            rf_passes.append((w_rf, c, w_rf_rows[:, :, k_cols]))
            rf_passes.append((x_rf, c, x_rf_rows[:, :, k_cols]))

        bb_chunks = []
        bb_passes = []
        for n in range(B * G // CHUNK):
            s, g0 = n // (G // BLOCKS), BLOCKS * (n % (G // BLOCKS))
            x = new_operand("x_bb%d" % n, 1)
            bb_chunks.append(
                {"x": x, "w": w_bb, "bias": 0, "sample_block": s, "first_group": g0}
            )
            bb_passes.append((x, 0, BB_feature[s * P : (s + 1) * P, g0 : g0 + BLOCKS, :]))

        quick, groups, start = [], [], 0
        for g, size in enumerate(GROUP_SIZES):
            if g < 2:
                quick.append(bb_chunks[start])
                start += 1
            groups.append(bb_chunks[start : start + size])
            start += size
        assert start == len(bb_chunks)
        n_first = 1 + GROUP_SIZES[0]
        for chunk in [rf_chunk] + quick:
            chunk["steep"], chunk["spare"] = steep, spare
        quick[0]["steep"], quick[0]["spare"] = steep_quick, spare_quick

        passes = [(w_bb, 0, W_bbbb.rearrange("(j p) k -> p j k", p=P))]
        passes = passes + bb_passes[:n_first] + rf_passes + bb_passes[n_first:]

        def product(bank, chunk, o):
            w, x = chunk["w"], chunk["x"]
            cols = slice(o * P, (o + 1) * P)
            for c in range(x["passes"]):
                nc.tensor.matmul_mx(
                    out=bank[:],
                    lhsT=w["codes"][:, c, cols].bitcast(FP8X4),
                    lhsT_scale=w["scales"][:, c, cols],
                    rhs=x["codes"][:, c, :].bitcast(FP8X4),
                    rhs_scale=x["scales"][:, c, :],
                    start=(c == 0),
                    stop=(c == x["passes"] - 1),
                )

        def sigmoid(chunk):
            if chunk is rf_chunk:
                act = consts.tile([P, BLOCKS, CHUNK], F32, name="rf_act")
            else:
                act = acts.tile([P, BLOCKS, CHUNK], F32, name="act")
            chunk["act"] = act
            for o in range(BLOCKS):
                bank = front.tile([P, CHUNK], F32, name="first")
                product(bank, chunk, o)
                col = slice(chunk["bias"] + o, chunk["bias"] + o + 1)
                nc.scalar.activation(
                    out=act[:, o, :], in_=bank[:], func=ACT.Sigmoid, bias=neg_bias[:, col], scale=-1.0
                )
                if "steep" in chunk:
                    nc.scalar.activation(
                        out=chunk["steep"][:, o, :], in_=bank[:], func=ACT.Sigmoid,
                        bias=steep_bias[:, col], scale=-4.0,
                    )

        def log(chunk):
            act = chunk["act"]
            nc.scalar.activation(
                out=act[:], in_=act[:], func=ACT.Ln, bias=guard[:, 0:1], scale=1.0
            )

        def tanh(chunk):
            act = chunk["act"]
            for h in range(HALF):
                half = act[:, 2 * h : 2 * h + 2, :]
                nc.scalar.activation(out=half, in_=half, func=ACT.Tanh, scale=-1.0)

        def tanh_without_log(chunk):
            fused = nc.vector.scalar_tensor_tensor
            parts = []
            for h in range(HALF):
                part = slice(2 * h, 2 * h + 2)
                parts.append(
                    (chunk["act"][:, part, :], chunk["steep"][:, part, :], chunk["spare"][:, part, :])
                )
            for s, d, v in parts:
                fused(out=v, in0=s, scalar=-0.8, in1=s, op0=ALU.add, op1=ALU.mult)
            for s, d, v in parts:
                fused(out=d, in0=v, scalar=0.2, in1=d, op0=ALU.add, op1=ALU.mult)
            for s, d, v in parts:
                fused(out=v, in0=d, scalar=-1.25, in1=v, op0=ALU.mult, op1=ALU.add)
            for s, d, v in parts:
                fused(out=s, in0=s, scalar=0.8, in1=v, op0=ALU.mult, op1=ALU.add)
            for s, d, v in parts:
                nc.vector.tensor_scalar(
                    out=s, in0=s, scalar1=-2.0, scalar2=1.0, op0=ALU.mult, op1=ALU.add
                )

        def tanh_on_gpsimd(chunk):
            for o in range(BLOCKS):
                s, d, v = chunk["act"][:, o, :], chunk["steep"][:, o, :], chunk["spare"][:, o, :]
                nc.gpsimd.tensor_tensor(out=v, in0=s, in1=s, op=ALU.mult)
                nc.gpsimd.tensor_scalar(
                    out=s, in0=s, scalar1=-0.8, scalar2=0.2, op0=ALU.mult, op1=ALU.add
                )
                nc.gpsimd.tensor_tensor(out=s, in0=s, in1=v, op=ALU.add)
                nc.gpsimd.tensor_tensor(out=d, in0=d, in1=s, op=ALU.mult)
                nc.gpsimd.tensor_scalar(
                    out=v, in0=v, scalar1=-2.0, scalar2=1.0, op0=ALU.mult, op1=ALU.add
                )
                nc.gpsimd.tensor_scalar(
                    out=d, in0=d, scalar1=2.5, scalar2=0.0, op0=ALU.mult, op1=ALU.add
                )
                nc.gpsimd.tensor_tensor(out=s, in0=v, in1=d, op=ALU.add)

        def times_z(chunk, h):
            act = chunk["act"]
            for o in range(2 * h, 2 * h + 2):
                bank = rest.tile([P, CHUNK], F32, name="bank")
                product(bank, chunk, o)
                col = chunk["bias"] + o
                nc.vector.scalar_tensor_tensor(
                    out=act[:, o, :], in0=bank[:], scalar=bias[:, col : col + 1],
                    in1=act[:, o, :], op0=ALU.add, op1=ALU.mult,
                )

        late = {}

        def turn_back(chunk, j, on_scalar):
            act, s = chunk["act"], chunk["sample_block"]
            bank = rest.tile([P, CHUNK], F32, name="bank")
            for o in range(BLOCKS):
                cols = slice(o * P, (o + 1) * P)
                nc.tensor.matmul(
                    bank[:, cols], lhsT=act[:, o, j * P : (j + 1) * P], rhs=ident[:],
                    is_transpose=True, start=True, stop=not on_scalar,
                )
                if on_scalar:
                    nc.tensor.matmul(
                        bank[:, cols], lhsT=rf_chunk["act"][:, o, s * P : (s + 1) * P],
                        rhs=ident[:], is_transpose=True, start=False, stop=True,
                    )
            if chunk is rf_chunk:
                nc.vector.tensor_copy(out=rf_to_bb[:, j, :], in_=bank[:])
                return
            stage = late["stages"].tile([P, DB], F32, name="stage")
            if on_scalar:
                nc.scalar.copy(out=stage[:], in_=bank[:])
            else:
                nc.vector.tensor_tensor(
                    out=stage[:], in0=bank[:], in1=rf_to_bb[:, s, :], op=ALU.add
                )
            nc.sync.dma_start(
                out=out[s * P : (s + 1) * P, chunk["first_group"] + j, :], in_=stage[:]
            )

        with ExitStack() as preparing:
            raws = preparing.enter_context(tc.tile_pool(name="raws", bufs=4))
            groupeds = preparing.enter_context(tc.tile_pool(name="groupeds", bufs=4))

            def start_pass(k):
                raw = raws.tile([P, BLOCKS, K_PASS], BF16, name="raw")
                grouped = groupeds.tile([P, CHUNK * PACK], BF16, name="grouped", align_bytes=64)
                return {"k": k, "raw": raw, "grouped": grouped}

            def load(item, blocks):
                nc.sync.dma_start(out=item["raw"][:, blocks, :], in_=passes[item["k"]][2][:, blocks, :])

            def regroup(item, j0, n, pool, name, copy):
                words = item["raw"][:].bitcast(F32)
                grouped_words = item["grouped"][:].bitcast(F32).rearrange(
                    "p (j r u) -> p j r u", j=BLOCKS, u=2
                )
                bank = pool.tile([P, CHUNK], F32, name=name)
                flipped = bank[:, 0 : n * 2 * P].rearrange("p (j u r) -> p j u r", j=n, u=2)
                for j in range(n):
                    for u in range(2):
                        nc.tensor.transpose(
                            flipped[:, j, u, :], words[:, j0 + j, u : 2 * P : 2], ident[:]
                        )
                copy(
                    out=grouped_words[:, j0 : j0 + n, :, :],
                    in_=flipped.rearrange("p j u r -> p j r u"),
                )

            def quantise(item, j0, n):
                operand, c = passes[item["k"]][0], passes[item["k"]][1]
                cols = slice(j0 * P, (j0 + n) * P)
                nc.vector.quantize_mx(
                    out=operand["codes"][:, c, cols].bitcast(FP8X4),
                    scales=operand["scales"][:, c, cols],
                    in_=item["grouped"][:, j0 * K_PASS : (j0 + n) * K_PASS],
                )

            vector_copy, scalar_copy = nc.vector.tensor_copy, nc.scalar.copy
            first_w, first_x = start_pass(0), start_pass(1)
            load_biases()
            load(first_w, slice(0, 1))
            for j in range(BLOCKS):
                load(first_x, slice(j, j + 1))
            for j in range(1, BLOCKS):
                load(first_w, slice(j, j + 1))
            turn_biases()
            regroup(first_w, 0, 1, rest, "bank", vector_copy)
            regroup(first_x, 0, 1, rest, "bank", scalar_copy)
            regroup(first_x, 1, 1, rest, "bank", vector_copy)
            quantise(first_w, 0, 1)
            regroup(first_x, 2, 1, rest, "bank", scalar_copy)
            regroup(first_x, 3, 1, rest, "bank", vector_copy)
            quantise(first_x, 0, BLOCKS)
            regroup(first_w, 1, 1, front, "first", vector_copy)
            for j in range(2, BLOCKS):
                regroup(first_w, j, 1, front, "first", vector_copy)
                quantise(first_w, j - 1, 1)
            quantise(first_w, BLOCKS - 1, 1)
            sigmoid(quick[0])
            tanh_on_gpsimd(quick[0])

            state = {"pending": None, "done": 2}

            def quantise_pending():
                if state["pending"] is not None:
                    quantise(state["pending"], 0, BLOCKS)
                    state["pending"] = None

            def prepare_up_to(n):
                while state["done"] < min(n, len(passes)):
                    item = start_pass(state["done"])
                    load(item, slice(0, BLOCKS))
                    for h in range(HALF):
                        regroup(item, 2 * h, 2, rest, "bank", vector_copy)
                    quantise_pending()
                    state["pending"] = item
                    state["done"] += 1

            n_needed = 1 + n_first + len(rf_passes)
            for i, chunk in enumerate([quick[0]] + groups[0] + [rf_chunk]):
                prepare_up_to(min(n_needed, LEAD + i + i // 3))
                if state["done"] == n_needed:
                    quantise_pending()
                if i > 0:
                    sigmoid(chunk)
            prepare_up_to(len(passes))
            quantise_pending()

        late["stages"] = ctx.enter_context(tc.tile_pool(name="stages", bufs=8))
        for g, group in enumerate(groups):
            following = groups[g + 1] if g + 1 < len(groups) else []
            if g == 0:
                following = [quick[1]] + following
            for chunk in group:
                log(chunk)
            if g == 0:
                tanh_without_log(rf_chunk)
                for h in range(HALF):
                    times_z(rf_chunk, h)
            call_in_sigmoid_table()
            previous = None
            if g < 2:
                for h in range(HALF):
                    times_z(quick[g], h)
                previous = quick[g]
            for i in range(len(group) + 1):
                if i < len(group):
                    tanh(group[i])
                if i < min(len(group), len(following)):
                    sigmoid(following[i])
                    if following[i] is quick[1]:
                        tanh_on_gpsimd(quick[1])
                if g == 0 and i == 0:
                    for j in range(BLOCKS):
                        turn_back(rf_chunk, j, False)
                shared = not following and i >= len(group) - 1
                for h in range(HALF):
                    if i < len(group):
                        times_z(group[i], h)
                    if previous is not None:
                        turn_back(previous, 2 * h, False)
                        turn_back(previous, 2 * h + 1, shared)
                previous = group[i] if i < len(group) else None
